import numpy as np
import ml_dtypes


def mxq(x, axis, fmt="e4m3"):
    dtype, down = {"e4m3": (ml_dtypes.float8_e4m3fn, 7), "e5m2": (ml_dtypes.float8_e5m2, 14)}[fmt]
    v = np.moveaxis(np.asarray(x, np.float32).astype(ml_dtypes.bfloat16).astype(np.float64), axis, -1)
    blocks = v.reshape(v.shape[:-1] + (-1, 32))
    amax = np.abs(blocks).max(-1, keepdims=True)
    byte = np.maximum(np.where(amax > 0, np.frexp(amax)[1] - 1 + 127, 0) - down, 1)
    scale = np.exp2(byte - 127.0)
    codes = (blocks / scale).astype(np.float32).astype(dtype).astype(np.float64)
    return np.moveaxis((codes * scale).reshape(v.shape), -1, axis)


WIDE = False


def mx_kscale(k):
    if not WIDE:
        return np.ones(k)
    levels = np.array([30, -30])
    if k % 512:
        return np.exp2(np.random.permutation(np.resize(levels, k // 32))).repeat(32)
    a = np.empty((k // 512, 16))
    for p in range(k // 512):
        a[p, :8] = np.random.permutation(np.resize(levels, 8))
        for g in range(8):
            far = levels[np.abs(levels - a[p, g]) >= 10]
            a[p, g + 8] = far[np.random.randint(len(far))]
    return np.exp2(a.ravel()).repeat(32)


BF16 = ml_dtypes.bfloat16


def bf(x):
    return np.asarray(x, np.float32).astype(BF16)


def f64(x):
    return np.asarray(x).astype(np.float64)


E2M1 = np.array([0.0, 0.5, 1.0, 1.5, 2.0, 3.0, 4.0, 6.0, -0.0, -0.5, -1.0, -1.5, -2.0, -3.0, -4.0, -6.0])


def pack_weight(w, fmt):
    k, n = w.shape
    w = f64(bf(w)).reshape(k // 32, 32, n)
    amax = np.abs(w).max(1)
    if fmt == "e4m3":
        byte = np.frexp(amax)[1] - 1 + 127 - 7
    else:
        mant, ex = np.frexp(amax / 6.0)
        byte = np.where(mant > 0.5, ex, ex - 1) + 127
    byte = np.clip(np.where(amax > 0, byte, 1), 1, 254)
    scaled = (w * np.exp2(127.0 - byte)[:, None, :]).reshape(k, n).astype(np.float32)
    by_word = np.ascontiguousarray(scaled.reshape(k // 512, 128, 4, n).transpose(0, 1, 3, 2))
    if fmt == "e4m3":
        words = by_word.astype(ml_dtypes.float8_e4m3fn).view(np.uint8)
    else:
        c = by_word.astype(ml_dtypes.float4_e2m1fn).view(np.uint8) & 0xF
        words = c[..., 0::2] | (c[..., 1::2] << 4)
    return np.ascontiguousarray(words), np.ascontiguousarray(byte.astype(np.uint8).reshape(k // 512, 16, n))


def unpack_weight(words, scales, fmt):
    g, p, n, _ = words.shape
    if fmt == "e4m3":
        vals = np.ascontiguousarray(words).view(ml_dtypes.float8_e4m3fn).astype(np.float64)
    else:
        nib = np.empty((g, p, n, 4), np.uint8)
        nib[..., 0::2] = words & 0xF
        nib[..., 1::2] = words >> 4
        vals = E2M1[nib]
    vals = vals * np.repeat(np.exp2(scales.astype(np.float64) - 127.0), 8, axis=1)[..., None]
    return vals.transpose(0, 1, 3, 2).reshape(g * 512, n)

def pack4(w):
    words, scales = pack_weight(w, "e2m1")
    return words.reshape(words.shape[0], 128, -1), scales


def unpack4(words, scales):
    return unpack_weight(words.reshape(words.shape[0], 128, -1, 2), scales, "e2m1")


B, S, HIDDEN, NH, NKV, HD, WINDOW = 1, 1024, 1024, 8, 4, 256, 512
Q_SIZE, KV_SIZE = NH * HD, NKV * HD
O_SIZE = Q_SIZE + KV_SIZE + KV_SIZE
EPS = 1e-6
ROPE_THETA = 10000.0


def rms_norm(u, w):
    var = np.mean(np.square(u), axis=-1, keepdims=True)
    return u / np.sqrt(var + EPS) * (1.0 + w)


def rope(u, cos, sin):
    d2 = u.shape[-1] // 2
    u1, u2 = u[..., :d2], u[..., d2:]
    c = cos[None, :, None, :]
    s = sin[None, :, None, :]
    return np.concatenate([u1 * c - u2 * s, u1 * s + u2 * c], axis=-1)


def setup_inputs():
    s = mx_kscale(HIDDEN)
    inv_freq = 1.0 / ROPE_THETA ** (np.arange(0, HD, 2) / HD)
    ang = np.arange(S)[:, None] * inv_freq[None, :]
    x = bf(np.random.standard_normal((B, S, HIDDEN)) * s)
    qkv_w = np.random.standard_normal((O_SIZE, HIDDEN)) / np.sqrt(HIDDEN) / s[None, :]
    words, scales = pack4(np.ascontiguousarray(qkv_w.T))
    return {"x": x,
            "qkv_w_words": words,
            "qkv_w_scales": scales,
            "q_norm_w": bf(1.0 + 0.3 * np.random.standard_normal(HD)),
            "k_norm_w": bf(1.0 + 0.3 * np.random.standard_normal(HD)),
            "freqs_cos": bf(np.cos(ang)),
            "freqs_sin": bf(np.sin(ang))}


def reference(x, qkv_w_words, qkv_w_scales, q_norm_w, k_norm_w, freqs_cos, freqs_sin):
    qkv = mxq(f64(x), 2, "e5m2") @ unpack4(qkv_w_words, qkv_w_scales)
    q = qkv[..., :Q_SIZE].reshape(B, S, NH, HD)
    k = qkv[..., Q_SIZE:Q_SIZE + KV_SIZE].reshape(B, S, NKV, HD)
    v = qkv[..., Q_SIZE + KV_SIZE:].reshape(B, S, NKV, HD)
    q = rms_norm(q, f64(q_norm_w))
    k = rms_norm(k, f64(k_norm_w))
    q = rope(q, f64(freqs_cos), f64(freqs_sin))
    k = rope(k, f64(freqs_cos), f64(freqs_sin))
    return q, k, v

@@ -1,0 +1,255 @@
+from contextlib import ExitStack
+
+import concourse.mybir as mybir
+from concourse.masks import make_identity
+
+F32 = mybir.dt.float32
+BF16 = mybir.dt.bfloat16
+I32 = mybir.dt.int32
+U32 = mybir.dt.uint32
+U8 = mybir.dt.uint8
+E5M2X4 = mybir.dt.float8_e5m2_x4
+E2M1X4 = mybir.dt.float4_e2m1fn_x4
+ALU = mybir.AluOpType
+ACT = mybir.ActivationFunctionType
+
+S, HIDDEN, HD = 1024, 1024, 256
+Q_SIZE, KV_SIZE = 2048, 1024
+O_SIZE = Q_SIZE + 2 * KV_SIZE
+EPS = 1e-6
+FLOPS = 2 * S * HIDDEN * O_SIZE
+
+P = 128
+HALF = HD // 2
+TILES = S // P
+PASSES = HIDDEN // 512
+BANK = 512
+QK_BANKS = (Q_SIZE + KV_SIZE) // BANK
+HEAD_TABLES = 2
+WORD_CHUNKS = [(0, 512), (512, 512), (1024, 512), (1536, 512), (2048, 1024), (3072, 1024)]
+SCALE_CHUNKS = [(0, 1024), (1024, 2048), (3072, 1024)]
+
+
+def tile_gemmaattention_pa_kernel(
+    tc, x, qkv_w_words, qkv_w_scales, q_norm_w, k_norm_w, freqs_cos, freqs_sin, out_0, out_1, out_2
+):
+    nc = tc.nc
+    x_rows = x[0].rearrange("(p i) k -> p i k", i=TILES)
+    cos_rows = freqs_cos.rearrange("(p i) d -> p i d", i=TILES)
+    sin_rows = freqs_sin.rearrange("(p i) d -> p i d", i=TILES)
+    q_rows = out_0[0].rearrange("(p i) h d -> p i (h d)", i=TILES)
+    k_rows = out_1[0].rearrange("(p i) h d -> p i (h d)", i=TILES)
+    v_rows = out_2[0].rearrange("(p i) h d -> p i (h d)", i=TILES)
+    late = TILES - HEAD_TABLES
+
+    with ExitStack() as ctx:
+        keep = ctx.enter_context(tc.tile_pool(name="keep", bufs=1))
+        work = ctx.enter_context(tc.tile_pool(name="work", bufs=3))
+        psum = ctx.enter_context(tc.psum_pool(name="psum", bufs=1))
+        ctx.enter_context(tc.manual_schedule())
+
+        ident = keep.tile([P, P], F32, name="ident")
+        ident4 = keep.tile([P, 4, P], BF16, name="ident4")
+        ones = keep.tile([P, P], BF16, name="ones")
+        gain_rows = keep.tile([P, 2 * HD], BF16, name="gain_rows")
+        diag_w = keep.tile([P, 4 * P], BF16, name="diag_w")
+        planes = [keep.tile([P, PASSES, n], U8, name="plane%d" % c, align_bytes=64) for c, (c0, n) in enumerate(SCALE_CHUNKS)]
+        words = [keep.tile([P, PASSES, 2 * n], U8, name="words%d" % c, align_bytes=64) for c, (c0, n) in enumerate(WORD_CHUNKS)]
+        x_sb = [keep.tile([P, HIDDEN], BF16, name="x%d" % i) for i in range(TILES)]
+        cos_early = keep.tile([P, HEAD_TABLES, HALF], BF16, name="cos_early")
+        sin_early = keep.tile([P, HEAD_TABLES, HALF], BF16, name="sin_early")
+        cos_late = keep.tile([P, late, HALF], BF16, name="cos_late")
+        sin_late = keep.tile([P, late, HALF], BF16, name="sin_late")
+        cos_t = keep.tile([P, late, P], BF16, name="cos_t")
+        sin_t = keep.tile([P, late, P], BF16, name="sin_t")
+        tables = [keep.tile([P, 2, 4, HALF], F32, name="table%d" % i) for i in range(TILES)]
+        x_mx = {}
+        v_out = {}
+
+        def qk_bank():
+            return psum.tile([P, BANK], F32, name="qk", tag="qk", bufs=5)
+
+        def side_bank(shape, dtype):
+            return psum.tile(shape, dtype, name="side", tag="side", bufs=3)
+
+        def load_words(c):
+            c0, n = WORD_CHUNKS[c]
+            src = qkv_w_words.rearrange("g p b -> p g b")[:, :, 2 * c0 : 2 * (c0 + n)]
+            nc.sync.dma_start(out=words[c][:].bitcast(I32), in_=src.bitcast(I32))
+
+        def load_scales(c):
+            c0, n = SCALE_CHUNKS[c]
+            for r in range(4):
+                src = qkv_w_scales[:, r:16:4, c0 : c0 + n].rearrange("g q n -> q g n")
+                nc.sync.dma_start(out=planes[c][r:P:32, :, :].bitcast(I32), in_=src.bitcast(I32))
+
+        def load_x(i):
+            nc.sync.dma_start(out=x_sb[i][:], in_=x_rows[:, i, :])
+
+        def weights(g, col):
+            w = [t[:, g, 2 * (col - c0) : 2 * (col - c0 + BANK)] for t, (c0, n) in zip(words, WORD_CHUNKS) if c0 <= col < c0 + n]
+            s = [t[:, g, col - c0 : col - c0 + BANK] for t, (c0, n) in zip(planes, SCALE_CHUNKS) if c0 <= col < c0 + n]
+            return w[0].bitcast(E2M1X4), s[0]
+
+        def project(i, col, bank):
+            for g in range(PASSES):
+                codes, scales = x_mx[i, g]
+                w, w_scale = weights(g, col)
+                nc.tensor.matmul_mx(
+                    out=bank[:], lhsT=codes.bitcast(E5M2X4), lhsT_scale=scales, rhs=w, rhs_scale=w_scale,
+                    start=(g == 0), stop=(g == PASSES - 1),
+                )
+
+        def turn_x(i, g0, n):
+            pairs = x_sb[i][:].bitcast(F32)
+            bank = side_bank([P, n, 2, P], F32)
+            for g in range(n):
+                for u in range(2):
+                    w0 = 256 * (g0 + g)
+                    nc.tensor.transpose(bank[:, g, u, :], pairs[:, w0 + u : w0 + 256 : 2], ident[:])
+            grouped = work.tile([P, n * 4 * P], BF16, name="grouped", tag="grouped", align_bytes=64)
+            nc.scalar.copy(
+                out=grouped[:].bitcast(F32).rearrange("p (g r u) -> p g r u", g=n, u=2),
+                in_=bank[:].rearrange("p g u r -> p g r u"),
+            )
+            return grouped
+
+        def quantize(i, g0, n, grouped):
+            codes = work.tile([P, n * P], U32, name="codes", tag="codes", align_bytes=64, bufs=4)
+            scales = work.tile([P, n * P], U8, name="scales", tag="scales", align_bytes=64, bufs=4)
+            nc.vector.quantize_mx(out=codes[:].bitcast(E5M2X4), scales=scales[:], in_=grouped[:])
+            for g in range(n):
+                x_mx[i, g0 + g] = (codes[:, g * P : (g + 1) * P], scales[:, g * P : (g + 1) * P])
+
+        def turn_freqs(src, dst):
+            bank = side_bank([P, late, P], BF16)
+            for t in range(late):
+                nc.tensor.transpose(bank[:, t, :], src[:, t, :], ident4[:, 0, :])
+            nc.scalar.copy(out=dst[:], in_=bank[:])
+
+        def gained(freq_t):
+            bank = side_bank([P, 2, 2, HALF], F32)
+            flat = bank[:].rearrange("p t h d -> p (t h d)")
+            nc.tensor.matmul(flat, lhsT=freq_t, rhs=ident4[:].rearrange("p c d -> p (c d)"), start=True, stop=False)
+            nc.tensor.matmul(flat, lhsT=freq_t, rhs=diag_w[:], start=False, stop=True)
+            return bank
+
+        def cos_table(i):
+            bank = gained(cos_t[:, i - HEAD_TABLES, :])
+            nc.scalar.copy(out=tables[i][:, :, 0:4:3, :], in_=bank[:])
+
+        def sin_table(i):
+            bank = gained(sin_t[:, i - HEAD_TABLES, :])
+            nc.scalar.copy(out=tables[i][:, :, 2, :], in_=bank[:, :, 0, :])
+            nc.scalar.activation(out=tables[i][:, :, 1, :], in_=bank[:, :, 1, :], func=ACT.Copy, scale=-1.0)
+
+        def values(i, c):
+            if c == 0:
+                v_out[i] = work.tile([P, KV_SIZE], F32, name="v_out", tag="v_out")
+            bank = side_bank([P, BANK], F32)
+            project(i, Q_SIZE + KV_SIZE + c * BANK, bank)
+            nc.scalar.copy(out=v_out[i][:, c * BANK : (c + 1) * BANK], in_=bank[:])
+            if c == 1:
+                nc.sync.dma_start(out=v_rows[:, i, :], in_=v_out[i][:])
+
+        def store(i, b0, n, src):
+            if b0 < Q_SIZE // BANK:
+                dst = q_rows[:, i, b0 * BANK : (b0 + n) * BANK]
+            else:
+                dst = k_rows[:, i, b0 * BANK - Q_SIZE : (b0 + n) * BANK - Q_SIZE]
+            nc.sync.dma_start(out=dst, in_=src)
+
+        nc.vector.memset(gain_rows[:], 0.0)
+        nc.vector.memset(planes[0][:].bitcast(I32), 0)
+        nc.vector.memset(gain_rows[32:33, :], 1.0)
+        nc.vector.memset(ones[:], 1.0)
+        nc.vector.memset(planes[1][:].bitcast(I32), 0)
+        nc.vector.memset(planes[2][:].bitcast(I32), 0)
+        make_identity(nc, ident[:])
+        nc.vector.tensor_copy(out=ident4[:], in_=ident[:].unsqueeze(1).to_broadcast([P, 4, P]))
+
+        nc.scalar.dma_start(out=gain_rows[0:1, 0:HD], in_=q_norm_w.rearrange("(o d) -> o d", o=1))
+        nc.scalar.dma_start(out=gain_rows[0:1, HD : 2 * HD], in_=k_norm_w.rearrange("(o d) -> o d", o=1))
+        load_x(0)
+        nc.sync.dma_start(out=cos_early[:], in_=cos_rows[:, :HEAD_TABLES, :])
+        nc.sync.dma_start(out=sin_early[:], in_=sin_rows[:, :HEAD_TABLES, :])
+        load_scales(0)
+        load_words(0)
+        load_words(1)
+        load_x(1)
+        load_scales(1)
+        load_words(2)
+        load_words(3)
+        load_words(4)
+        load_scales(2)
+        load_words(5)
+        nc.sync.dma_start(out=cos_late[:], in_=cos_rows[:, HEAD_TABLES:, :])
+        nc.sync.dma_start(out=sin_late[:], in_=sin_rows[:, HEAD_TABLES:, :])
+        for i in range(2, TILES):
+            load_x(i)
+
+        gains = qk_bank()
+        nc.tensor.matmul(gains[:], lhsT=ones[:], rhs=gain_rows[:], start=True, stop=True)
+        gains4 = gains[:].rearrange("p (t h d) -> p t h d", t=2, h=2)
+        first = [turn_x(0, g, 1) for g in range(PASSES)]
+        for g in range(PASSES):
+            quantize(0, g, 1, first[g])
+        for i in range(HEAD_TABLES):
+            c = cos_early[:, i, :].unsqueeze(1).unsqueeze(1).to_broadcast([P, 2, 2, HALF])
+            s = sin_early[:, i, :].unsqueeze(1).to_broadcast([P, 2, HALF])
+            nc.vector.tensor_tensor(out=tables[i][:, :, 0:4:3, :], in0=gains4, in1=c, op=ALU.mult)
+            nc.vector.tensor_tensor(out=tables[i][:, :, 2, :], in0=gains4[:, :, 0, :], in1=s, op=ALU.mult)
+            nc.vector.scalar_tensor_tensor(
+                out=tables[i][:, :, 1, :], in0=gains4[:, :, 1, :], scalar=-1.0, in1=s, op0=ALU.mult, op1=ALU.mult
+            )
+        nc.vector.scalar_tensor_tensor(
+            out=diag_w[:], in0=gains[:], scalar=-1.0, in1=ident4[:].rearrange("p c d -> p (c d)"), op0=ALU.add, op1=ALU.mult
+        )
+
+        for i in range(TILES):
+            last = i == TILES - 1
+            group = 1 if i == 0 or last else 2
+            grouped = None
+            for b in range(QK_BANKS):
+                bank = qk_bank()
+                project(i, b * BANK, bank)
+                sums = work.tile([P, 2], F32, name="sums", tag="sums", bufs=6)
+                for h in range(2):
+                    squares = work.tile([P, HD], BF16, name="squares", tag="squares")
+                    nc.scalar.activation(
+                        out=squares[:], in_=bank[:, h * HD : (h + 1) * HD], func=ACT.Square, accum_out=sums[:, h : h + 1]
+                    )
+
+                if b == 0 and i == 1:
+                    turn_freqs(cos_late, cos_t)
+                    turn_freqs(sin_late, sin_t)
+                if b == 1 and not last:
+                    grouped = turn_x(i + 1, 0, PASSES)
+                if b == 2 and HEAD_TABLES <= i + 1 < TILES:
+                    cos_table(i + 1)
+                if b == 3 and HEAD_TABLES <= i + 1 < TILES:
+                    sin_table(i + 1)
+                if b - (1 if last else 4) in (0, 1):
+                    values(i, b - (1 if last else 4))
+
+                rstd = work.tile([P, 2], F32, name="rstd", tag="rstd", bufs=6)
+                nc.scalar.activation(out=rstd[:], in_=sums[:], func=ACT.Abs_reciprocal_sqrt, scale=1.0 / HD, bias=EPS)
+
+                if b % group == 0:
+                    terms = work.tile([P, 2 * group, 2, HD], F32, name="terms", tag="terms")
+                table = tables[i][:, 0 if b < Q_SIZE // BANK else 1, :, :].rearrange("p (j h) d -> p j (h d)", j=2)
+                for h in range(2):
+                    nc.vector.scalar_tensor_tensor(
+                        out=terms[:, 2 * (b % group) + h, :, :],
+                        in0=bank[:, h * HD : (h + 1) * HD].unsqueeze(1).to_broadcast([P, 2, HD]),
+                        scalar=rstd[:, h : h + 1], in1=table, op0=ALU.mult, op1=ALU.mult,
+                    )
+                if b == 1 and not last:
+                    quantize(i + 1, 0, PASSES, grouped)
+
+                if b % group == group - 1:
+                    result = work.tile([P, 4 * group, HALF], F32, name="result", tag="result", bufs=4)
+                    halves = terms[:].rearrange("p n j (h d) -> p (n j) h d", h=2)
+                    adder = nc.vector if last and b == QK_BANKS - 1 else nc.gpsimd
+                    adder.tensor_tensor(out=result[:], in0=halves[:, :, 0, :], in1=halves[:, :, 1, :], op=ALU.add)
+                    store(i, b - group + 1, group, result[:].rearrange("p n d -> p (n d)"))

@@ -24,9 +24,11 @@ HALF = HD // 2
 TILES = S // P
 PASSES = HIDDEN // 512
 BANK = 512
-QK_BANKS = (Q_SIZE + KV_SIZE) // BANK
-HEAD_TABLES = 2
-WORD_CHUNKS = [(0, 512), (512, 512), (1024, 512), (1536, 512), (2048, 1024), (3072, 1024)]
+STEPS = (Q_SIZE + KV_SIZE) // BANK
+QK_BANKS = 5
+QUANTISE_STEP = 3
+VECTOR_TAIL = 3
+WORD_CHUNKS = [(0, 512), (512, 512), (1024, 1024), (2048, 1024), (3072, 1024)]
 SCALE_CHUNKS = [(0, 1024), (1024, 2048), (3072, 1024)]
 
 
@@ -40,7 +42,6 @@ def tile_gemmaattention_pa_kernel(
     q_rows = out_0[0].rearrange("(p i) h d -> p i (h d)", i=TILES)
     k_rows = out_1[0].rearrange("(p i) h d -> p i (h d)", i=TILES)
     v_rows = out_2[0].rearrange("(p i) h d -> p i (h d)", i=TILES)
-    late = TILES - HEAD_TABLES
 
     with ExitStack() as ctx:
         keep = ctx.enter_context(tc.tile_pool(name="keep", bufs=1))
@@ -49,28 +50,39 @@ def tile_gemmaattention_pa_kernel(
         ctx.enter_context(tc.manual_schedule())
 
         ident = keep.tile([P, P], F32, name="ident")
-        ident4 = keep.tile([P, 4, P], BF16, name="ident4")
+        ident4 = keep.tile([P, 4 * P], BF16, name="ident4")
         ones = keep.tile([P, P], BF16, name="ones")
         gain_rows = keep.tile([P, 2 * HD], BF16, name="gain_rows")
         diag_w = keep.tile([P, 4 * P], BF16, name="diag_w")
-        planes = [keep.tile([P, PASSES, n], U8, name="plane%d" % c, align_bytes=64) for c, (c0, n) in enumerate(SCALE_CHUNKS)]
-        words = [keep.tile([P, PASSES, 2 * n], U8, name="words%d" % c, align_bytes=64) for c, (c0, n) in enumerate(WORD_CHUNKS)]
-        x_sb = [keep.tile([P, HIDDEN], BF16, name="x%d" % i) for i in range(TILES)]
-        cos_early = keep.tile([P, HEAD_TABLES, HALF], BF16, name="cos_early")
-        sin_early = keep.tile([P, HEAD_TABLES, HALF], BF16, name="sin_early")
-        cos_late = keep.tile([P, late, HALF], BF16, name="cos_late")
-        sin_late = keep.tile([P, late, HALF], BF16, name="sin_late")
-        cos_t = keep.tile([P, late, P], BF16, name="cos_t")
-        sin_t = keep.tile([P, late, P], BF16, name="sin_t")
+        planes = [keep.tile([P, PASSES, n], U8, name="plane%d" % c0, align_bytes=64) for c0, n in SCALE_CHUNKS]
+        words = [keep.tile([P, PASSES, 2 * n], U8, name="words%d" % c0, align_bytes=64) for c0, n in WORD_CHUNKS]
         tables = [keep.tile([P, 2, 4, HALF], F32, name="table%d" % i) for i in range(TILES)]
+        x_sb = {}
+        freq_sb = {}
+        freq_t = {}
         x_mx = {}
         v_out = {}
+        stores = []
 
         def qk_bank():
-            return psum.tile([P, BANK], F32, name="qk", tag="qk", bufs=5)
+            return psum.tile([P, BANK], F32, name="qk", tag="qk", bufs=QK_BANKS)
 
         def side_bank(shape, dtype):
-            return psum.tile(shape, dtype, name="side", tag="side", bufs=3)
+            return psum.tile(shape, dtype, name="side", tag="side", bufs=8 - QK_BANKS)
+
+        def load_x(i0, n):
+            rows = keep.tile([P, n, HIDDEN], BF16, name="x%d" % i0)
+            nc.sync.dma_start(out=rows[:], in_=x_rows[:, i0 : i0 + n, :])
+            for t in range(n):
+                x_sb[i0 + t] = rows[:, t, :]
+
+        def load_freqs(i0, n):
+            cos = keep.tile([P, n, HALF], BF16, name="cos%d" % i0)
+            sin = keep.tile([P, n, HALF], BF16, name="sin%d" % i0)
+            nc.sync.dma_start(out=cos[:], in_=cos_rows[:, i0 : i0 + n, :])
+            nc.sync.dma_start(out=sin[:], in_=sin_rows[:, i0 : i0 + n, :])
+            for t in range(n):
+                freq_sb[i0 + t] = (cos[:, t, :], sin[:, t, :])
 
         def load_words(c):
             c0, n = WORD_CHUNKS[c]
@@ -83,173 +95,242 @@ def tile_gemmaattention_pa_kernel(
                 src = qkv_w_scales[:, r:16:4, c0 : c0 + n].rearrange("g q n -> q g n")
                 nc.sync.dma_start(out=planes[c][r:P:32, :, :].bitcast(I32), in_=src.bitcast(I32))
 
-        def load_x(i):
-            nc.sync.dma_start(out=x_sb[i][:], in_=x_rows[:, i, :])
+        def chunk_of(tiles, chunks, col):
+            return [(t, col - c0) for t, (c0, n) in zip(tiles, chunks) if c0 <= col < c0 + n][0]
 
-        def weights(g, col):
-            w = [t[:, g, 2 * (col - c0) : 2 * (col - c0 + BANK)] for t, (c0, n) in zip(words, WORD_CHUNKS) if c0 <= col < c0 + n]
-            s = [t[:, g, col - c0 : col - c0 + BANK] for t, (c0, n) in zip(planes, SCALE_CHUNKS) if c0 <= col < c0 + n]
-            return w[0].bitcast(E2M1X4), s[0]
-
-        def project(i, col, bank):
+        def project(i, col, width, bank):
+            word_tile, w0 = chunk_of(words, WORD_CHUNKS, col)
+            plane, s0 = chunk_of(planes, SCALE_CHUNKS, col)
             for g in range(PASSES):
                 codes, scales = x_mx[i, g]
-                w, w_scale = weights(g, col)
                 nc.tensor.matmul_mx(
-                    out=bank[:], lhsT=codes.bitcast(E5M2X4), lhsT_scale=scales, rhs=w, rhs_scale=w_scale,
-                    start=(g == 0), stop=(g == PASSES - 1),
+                    out=bank[:, :width],
+                    lhsT=codes.bitcast(E5M2X4),
+                    lhsT_scale=scales,
+                    rhs=word_tile[:, g, 2 * w0 : 2 * (w0 + width)].bitcast(E2M1X4),
+                    rhs_scale=plane[:, g, s0 : s0 + width],
+                    start=(g == 0),
+                    stop=(g == PASSES - 1),
                 )
 
-        def turn_x(i, g0, n):
-            pairs = x_sb[i][:].bitcast(F32)
+        def turn_x(i, g0, n, grouped):
+            pairs = x_sb[i].bitcast(F32)
             bank = side_bank([P, n, 2, P], F32)
             for g in range(n):
                 for u in range(2):
                     w0 = 256 * (g0 + g)
                     nc.tensor.transpose(bank[:, g, u, :], pairs[:, w0 + u : w0 + 256 : 2], ident[:])
-            grouped = work.tile([P, n * 4 * P], BF16, name="grouped", tag="grouped", align_bytes=64)
             nc.scalar.copy(
-                out=grouped[:].bitcast(F32).rearrange("p (g r u) -> p g r u", g=n, u=2),
+                out=grouped.bitcast(F32).rearrange("p (g r u) -> p g r u", g=n, u=2),
                 in_=bank[:].rearrange("p g u r -> p g r u"),
             )
-            return grouped
 
-        def quantize(i, g0, n, grouped):
-            codes = work.tile([P, n * P], U32, name="codes", tag="codes", align_bytes=64, bufs=4)
-            scales = work.tile([P, n * P], U8, name="scales", tag="scales", align_bytes=64, bufs=4)
+        def new_grouped(n):
+            return work.tile([P, n * 4 * P], BF16, name="grouped", tag="grouped", align_bytes=64)
+
+        def quantize(keys, grouped):
+            n = len(keys)
+            codes = work.tile([P, n * P], U32, name="codes", tag="codes", align_bytes=64, bufs=5)
+            scales = work.tile([P, n * P], U8, name="scales", tag="scales", align_bytes=64, bufs=5)
             nc.vector.quantize_mx(out=codes[:].bitcast(E5M2X4), scales=scales[:], in_=grouped[:])
-            for g in range(n):
-                x_mx[i, g0 + g] = (codes[:, g * P : (g + 1) * P], scales[:, g * P : (g + 1) * P])
+            for j, key in enumerate(keys):
+                x_mx[key] = (codes[:, j * P : (j + 1) * P], scales[:, j * P : (j + 1) * P])
 
-        def turn_freqs(src, dst):
-            bank = side_bank([P, late, P], BF16)
-            for t in range(late):
-                nc.tensor.transpose(bank[:, t, :], src[:, t, :], ident4[:, 0, :])
-            nc.scalar.copy(out=dst[:], in_=bank[:])
+        def turn_freqs(a):
+            sources = freq_sb[a] + freq_sb[a + 1]
+            bank = side_bank([P, 4, P], BF16)
+            for j, src in enumerate(sources):
+                nc.tensor.transpose(bank[:, j, :], src, ident4[:, :P])
+            turned = keep.tile([P, 4, P], BF16, name="freq_t%d" % a)
+            nc.scalar.copy(out=turned[:], in_=bank[:])
+            for t in range(2):
+                freq_t[a + t] = (turned[:, 2 * t, :], turned[:, 2 * t + 1, :])
 
-        def gained(freq_t):
+        def times_gains(turned):
             bank = side_bank([P, 2, 2, HALF], F32)
             flat = bank[:].rearrange("p t h d -> p (t h d)")
-            nc.tensor.matmul(flat, lhsT=freq_t, rhs=ident4[:].rearrange("p c d -> p (c d)"), start=True, stop=False)
-            nc.tensor.matmul(flat, lhsT=freq_t, rhs=diag_w[:], start=False, stop=True)
+            nc.tensor.matmul(flat, lhsT=turned, rhs=ident4[:], start=True, stop=False)
+            nc.tensor.matmul(flat, lhsT=turned, rhs=diag_w[:], start=False, stop=True)
             return bank
 
-        def cos_table(i):
-            bank = gained(cos_t[:, i - HEAD_TABLES, :])
+        def cos_factors(i):
+            bank = times_gains(freq_t[i][0])
             nc.scalar.copy(out=tables[i][:, :, 0:4:3, :], in_=bank[:])
 
-        def sin_table(i):
-            bank = gained(sin_t[:, i - HEAD_TABLES, :])
+        def sin_factors(i):
+            bank = times_gains(freq_t[i][1])
             nc.scalar.copy(out=tables[i][:, :, 2, :], in_=bank[:, :, 0, :])
             nc.scalar.activation(out=tables[i][:, :, 1, :], in_=bank[:, :, 1, :], func=ACT.Copy, scale=-1.0)
 
-        def values(i, c):
-            if c == 0:
-                v_out[i] = work.tile([P, KV_SIZE], F32, name="v_out", tag="v_out")
-            bank = side_bank([P, BANK], F32)
-            project(i, Q_SIZE + KV_SIZE + c * BANK, bank)
-            nc.scalar.copy(out=v_out[i][:, c * BANK : (c + 1) * BANK], in_=bank[:])
-            if c == 1:
-                nc.sync.dma_start(out=v_rows[:, i, :], in_=v_out[i][:])
-
-        def store(i, b0, n, src):
-            if b0 < Q_SIZE // BANK:
-                dst = q_rows[:, i, b0 * BANK : (b0 + n) * BANK]
-            else:
-                dst = k_rows[:, i, b0 * BANK - Q_SIZE : (b0 + n) * BANK - Q_SIZE]
-            nc.sync.dma_start(out=dst, in_=src)
-
-        nc.vector.memset(gain_rows[:], 0.0)
-        nc.vector.memset(planes[0][:].bitcast(I32), 0)
-        nc.vector.memset(gain_rows[32:33, :], 1.0)
-        nc.vector.memset(ones[:], 1.0)
-        nc.vector.memset(planes[1][:].bitcast(I32), 0)
-        nc.vector.memset(planes[2][:].bitcast(I32), 0)
-        make_identity(nc, ident[:])
-        nc.vector.tensor_copy(out=ident4[:], in_=ident[:].unsqueeze(1).to_broadcast([P, 4, P]))
-
-        nc.scalar.dma_start(out=gain_rows[0:1, 0:HD], in_=q_norm_w.rearrange("(o d) -> o d", o=1))
-        nc.scalar.dma_start(out=gain_rows[0:1, HD : 2 * HD], in_=k_norm_w.rearrange("(o d) -> o d", o=1))
-        load_x(0)
-        nc.sync.dma_start(out=cos_early[:], in_=cos_rows[:, :HEAD_TABLES, :])
-        nc.sync.dma_start(out=sin_early[:], in_=sin_rows[:, :HEAD_TABLES, :])
-        load_scales(0)
-        load_words(0)
-        load_words(1)
-        load_x(1)
-        load_scales(1)
-        load_words(2)
-        load_words(3)
-        load_words(4)
-        load_scales(2)
-        load_words(5)
-        nc.sync.dma_start(out=cos_late[:], in_=cos_rows[:, HEAD_TABLES:, :])
-        nc.sync.dma_start(out=sin_late[:], in_=sin_rows[:, HEAD_TABLES:, :])
-        for i in range(2, TILES):
-            load_x(i)
-
-        gains = qk_bank()
-        nc.tensor.matmul(gains[:], lhsT=ones[:], rhs=gain_rows[:], start=True, stop=True)
-        gains4 = gains[:].rearrange("p (t h d) -> p t h d", t=2, h=2)
-        first = [turn_x(0, g, 1) for g in range(PASSES)]
-        for g in range(PASSES):
-            quantize(0, g, 1, first[g])
-        for i in range(HEAD_TABLES):
-            c = cos_early[:, i, :].unsqueeze(1).unsqueeze(1).to_broadcast([P, 2, 2, HALF])
-            s = sin_early[:, i, :].unsqueeze(1).to_broadcast([P, 2, HALF])
+        def table_on_vector(i, gains):
+            gains4 = gains[:].rearrange("p (t h d) -> p t h d", t=2, h=2)
+            c = freq_sb[i][0].unsqueeze(1).unsqueeze(1).to_broadcast([P, 2, 2, HALF])
+            s = freq_sb[i][1].unsqueeze(1).to_broadcast([P, 2, HALF])
             nc.vector.tensor_tensor(out=tables[i][:, :, 0:4:3, :], in0=gains4, in1=c, op=ALU.mult)
             nc.vector.tensor_tensor(out=tables[i][:, :, 2, :], in0=gains4[:, :, 0, :], in1=s, op=ALU.mult)
             nc.vector.scalar_tensor_tensor(
                 out=tables[i][:, :, 1, :], in0=gains4[:, :, 1, :], scalar=-1.0, in1=s, op0=ALU.mult, op1=ALU.mult
             )
-        nc.vector.scalar_tensor_tensor(
-            out=diag_w[:], in0=gains[:], scalar=-1.0, in1=ident4[:].rearrange("p c d -> p (c d)"), op0=ALU.add, op1=ALU.mult
+
+        def values(i, c):
+            if c == 0:
+                v_out[i] = work.tile([P, KV_SIZE], F32, name="v_out", tag="v_out", bufs=4)
+            bank = side_bank([P, BANK], F32)
+            project(i, Q_SIZE + KV_SIZE + c * BANK, BANK, bank)
+            nc.scalar.copy(out=v_out[i][:, c * BANK : (c + 1) * BANK], in_=bank[:])
+            if c == 1:
+                nc.sync.dma_start(out=v_rows[:, i, :], in_=v_out[i][:])
+
+        def new_sums(heads):
+            return work.tile([P, heads], F32, name="sums", tag="sums", bufs=4)
+
+        def square(bank, h, sums):
+            squares = work.tile([P, HD], BF16, name="squares", tag="squares")
+            nc.scalar.activation(
+                out=squares[:], in_=bank[:, h * HD : (h + 1) * HD], func=ACT.Square, accum_out=sums[:, h : h + 1]
+            )
+
+        def inverse_rms(sums):
+            rstd = work.tile([P, sums.shape[1]], F32, name="rstd", tag="rstd", bufs=4)
+            nc.scalar.activation(out=rstd[:], in_=sums[:], func=ACT.Abs_reciprocal_sqrt, scale=1.0 / HD, bias=EPS)
+            return rstd
+
+        def new_terms(tiles, heads):
+            return work.tile([P, tiles, heads, 2, HD], F32, name="terms", tag="terms", bufs=5)
+
+        def multiply(i, col, bank, h, rstd, terms):
+            table = tables[i][:, 0 if col < Q_SIZE else 1, :, :].rearrange("p (j h) d -> p j (h d)", j=2)
+            u = bank[:, h * HD : (h + 1) * HD].unsqueeze(1).to_broadcast([P, 2, HD])
+            nc.vector.scalar_tensor_tensor(out=terms, in0=u, scalar=rstd, in1=table, op0=ALU.mult, op1=ALU.mult)
+
+        def add(engine, i, col, terms):
+            tiles, heads = terms.shape[1], terms.shape[2]
+            result = work.tile([P, tiles * heads * 2, HALF], F32, name="result", tag="result", bufs=8)
+            halves = terms.rearrange("p t n j (h d) -> p (t n j) h d", h=2)
+            engine.tensor_tensor(out=result[:], in0=halves[:, :, 0, :], in1=halves[:, :, 1, :], op=ALU.add)
+            if col < Q_SIZE:
+                dst = q_rows[:, i : i + tiles, col : col + heads * HD]
+            else:
+                dst = k_rows[:, i : i + tiles, col - Q_SIZE : col - Q_SIZE + heads * HD]
+            stores.append((dst, result[:].rearrange("p (t n) d -> p t (n d)", t=tiles)))
+
+        def flush(keep_last):
+            while len(stores) > keep_last:
+                dst, src = stores[0]
+                nc.sync.dma_start(out=dst, in_=src)
+                stores.remove(stores[0])
+
+        def finish_unit(i, col, heads, sums, bank):
+            rstd = inverse_rms(sums)
+            terms = new_terms(1, heads)
+            for h in range(heads):
+                multiply(i, col, bank, h, rstd[:, h : h + 1], terms[:, 0, h, :, :])
+            add(nc.gpsimd, i, col, terms[:])
+
+        nc.scalar.dma_start(out=gain_rows[P - 1 : P, 0:HD], in_=q_norm_w.rearrange("(o d) -> o d", o=1))
+        nc.scalar.dma_start(out=gain_rows[P - 1 : P, HD : 2 * HD], in_=k_norm_w.rearrange("(o d) -> o d", o=1))
+        nc.vector.memset(planes[0][:].bitcast(I32), 0)
+        nc.vector.memset(gain_rows[: P - 1, :], 0.0)
+        nc.vector.memset(ones[:], 1.0)
+        nc.vector.memset(gain_rows[0:1, :], 1.0)
+        make_identity(nc, ident[:])
+        nc.vector.tensor_copy(
+            out=ident4[:].rearrange("p (c d) -> p c d", c=4), in_=ident[:].unsqueeze(1).to_broadcast([P, 4, P])
         )
+        for plane in planes[1:]:
+            nc.vector.memset(plane[:].bitcast(I32), 0)
 
-        for i in range(TILES):
-            last = i == TILES - 1
-            group = 1 if i == 0 or last else 2
-            grouped = None
-            for b in range(QK_BANKS):
-                bank = qk_bank()
-                project(i, b * BANK, bank)
-                sums = work.tile([P, 2], F32, name="sums", tag="sums", bufs=6)
-                for h in range(2):
-                    squares = work.tile([P, HD], BF16, name="squares", tag="squares")
-                    nc.scalar.activation(
-                        out=squares[:], in_=bank[:, h * HD : (h + 1) * HD], func=ACT.Square, accum_out=sums[:, h : h + 1]
-                    )
+        load_x(0, 1)
+        load_freqs(0, 2)
+        load_x(1, 1)
+        load_scales(0)
+        load_words(0)
+        load_words(1)
+        load_scales(1)
+        load_words(2)
+        load_x(2, 2)
+        load_freqs(2, TILES - 2)
+        load_words(3)
+        load_scales(2)
+        load_words(4)
 
-                if b == 0 and i == 1:
-                    turn_freqs(cos_late, cos_t)
-                    turn_freqs(sin_late, sin_t)
-                if b == 1 and not last:
-                    grouped = turn_x(i + 1, 0, PASSES)
-                if b == 2 and HEAD_TABLES <= i + 1 < TILES:
-                    cos_table(i + 1)
-                if b == 3 and HEAD_TABLES <= i + 1 < TILES:
-                    sin_table(i + 1)
-                if b - (1 if last else 4) in (0, 1):
-                    values(i, b - (1 if last else 4))
+        gains = qk_bank()
+        nc.tensor.matmul(gains[:], lhsT=ones[:], rhs=gain_rows[:], start=True, stop=True)
+        first = [new_grouped(1) for g in range(PASSES)]
+        second = new_grouped(PASSES)
+        for g in range(PASSES):
+            turn_x(0, g, 1, first[g][:])
+        turn_x(1, 0, PASSES, second[:])
+        nc.vector.scalar_tensor_tensor(
+            out=diag_w[:], in0=gains[:], scalar=-1.0, in1=ident4[:], op0=ALU.add, op1=ALU.mult
+        )
+        for g in range(PASSES):
+            quantize([(0, g)], first[g])
+        table_on_vector(0, gains)
+        quantize([(1, g) for g in range(PASSES)], second)
+        table_on_vector(1, gains)
 
-                rstd = work.tile([P, 2], F32, name="rstd", tag="rstd", bufs=6)
-                nc.scalar.activation(out=rstd[:], in_=sums[:], func=ACT.Abs_reciprocal_sqrt, scale=1.0 / HD, bias=EPS)
+        pending = []
+        for i, col, heads in [(0, 0, 1), (0, HD, 1), (1, 0, 2)]:
+            sums = new_sums(heads)
+            bank = qk_bank()
+            project(i, col, heads * HD, bank)
+            for h in range(heads):
+                square(bank, h, sums)
+                for unit in pending:
+                    finish_unit(*unit)
+                pending = []
+            pending = [(i, col, heads, sums, bank)]
+            if col == 0 and i == 0:
+                finish_unit(*pending[0])
+                pending = []
 
-                if b % group == 0:
-                    terms = work.tile([P, 2 * group, 2, HD], F32, name="terms", tag="terms")
-                table = tables[i][:, 0 if b < Q_SIZE // BANK else 1, :, :].rearrange("p (j h) d -> p j (h d)", j=2)
-                for h in range(2):
-                    nc.vector.scalar_tensor_tensor(
-                        out=terms[:, 2 * (b % group) + h, :, :],
-                        in0=bank[:, h * HD : (h + 1) * HD].unsqueeze(1).to_broadcast([P, 2, HD]),
-                        scalar=rstd[:, h : h + 1], in1=table, op0=ALU.mult, op1=ALU.mult,
-                    )
-                if b == 1 and not last:
-                    quantize(i + 1, 0, PASSES, grouped)
+        for a in range(0, TILES, 2):
+            last = a == TILES - 2
+            if a + 4 < TILES:
+                load_x(a + 4, 2)
+            side = [None]
+            side += [(values, a - 2 + t, c) if a > 0 else None for t in range(2) for c in range(2)]
+            if last:
+                side += [(values, a + t, c) for t in range(2) for c in range(2)]
+                side += [None] * (2 * STEPS - len(side))
+            else:
+                grouped = new_grouped(2 * PASSES)
+                side += [(turn_x, a + 2 + t, 0, PASSES, grouped[:, t * HIDDEN : (t + 1) * HIDDEN]) for t in range(2)]
+                side += [(turn_freqs, a + 2)]
+                side += [(make, a + 2 + t) for t in range(2) for make in (cos_factors, sin_factors)]
+            tail = []
+            for b in range(1 if a == 0 else 0, STEPS):
+                col = b * BANK
+                sums = new_sums(4)
+                banks = []
+                for t in range(2):
+                    banks.append(qk_bank())
+                    project(a + t, col, BANK, banks[t])
+                    for h in range(2):
+                        square(banks[t], h, sums[:, 2 * t : 2 * t + 2])
+                        for unit in pending:
+                            finish_unit(*unit)
+                        pending = []
+                    job = side[2 * b + t]
+                    if job is not None:
+                        job[0](*job[1:])
+                rstd = inverse_rms(sums)
+                flush(1)
+                terms = new_terms(2, 2)
+                on_gpsimd = min(2, max(0, 2 * STEPS - VECTOR_TAIL - 2 * b)) if last else 2
+                for t in range(2):
+                    for h in range(2):
+                        multiply(a + t, col, banks[t], h, rstd[:, 2 * t + h : 2 * t + h + 1], terms[:, t, h, :, :])
+                    if t >= on_gpsimd:
+                        tail.append((a + t, col, terms[:, t : t + 1, :, :, :]))
+                    elif t == on_gpsimd - 1:
+                        if b == QUANTISE_STEP and not last:
+                            quantize([(a + 2 + j, g) for j in range(2) for g in range(PASSES)], grouped)
+                        add(nc.gpsimd, a, col, terms[:, :on_gpsimd, :, :, :])
 
-                if b % group == group - 1:
-                    result = work.tile([P, 4 * group, HALF], F32, name="result", tag="result", bufs=4)
-                    halves = terms[:].rearrange("p n j (h d) -> p (n j) h d", h=2)
-                    adder = nc.vector if last and b == QK_BANKS - 1 else nc.gpsimd
-                    adder.tensor_tensor(out=result[:], in0=halves[:, :, 0, :], in1=halves[:, :, 1, :], op=ALU.add)
-                    store(i, b - group + 1, group, result[:].rearrange("p n d -> p (n d)"))
+        i, col, terms = tail[-1]
+        tail = tail[:-1] + [(i, col + h * HD, terms[:, :, h : h + 1, :, :]) for h in range(2)]
+        for part in tail:
+            add(nc.vector, *part)
+            flush(0)

@@ -128,6 +128,9 @@ def tile_gemmaattention_pa_kernel(
         def new_grouped(n):
             return work.tile([P, n * 4 * P], BF16, name="grouped", tag="grouped", align_bytes=64)
 
+        def shared_tile(shape, dtype):
+            return work.tile(shape, dtype, name="shared", tag="shared", align_bytes=64, bufs=1)
+
         def quantize(keys, grouped):
             n = len(keys)
             codes = work.tile([P, n * P], U32, name="codes", tag="codes", align_bytes=64, bufs=5)
@@ -203,9 +206,13 @@ def tile_gemmaattention_pa_kernel(
             u = bank[:, h * HD : (h + 1) * HD].unsqueeze(1).to_broadcast([P, 2, HD])
             nc.vector.scalar_tensor_tensor(out=terms, in0=u, scalar=rstd, in1=table, op0=ALU.mult, op1=ALU.mult)
 
-        def add(engine, i, col, terms):
+        def add(engine, i, col, terms, after_quantise=False):
             tiles, heads = terms.shape[1], terms.shape[2]
-            result = work.tile([P, tiles * heads * 2, HALF], F32, name="result", tag="result", bufs=8)
+            shape = [P, tiles * heads * 2, HALF]
+            if after_quantise:
+                result = shared_tile(shape, F32)
+            else:
+                result = work.tile(shape, F32, name="result", tag="result", bufs=8)
             halves = terms.rearrange("p t n j (h d) -> p (t n j) h d", h=2)
             engine.tensor_tensor(out=result[:], in0=halves[:, :, 0, :], in1=halves[:, :, 1, :], op=ALU.add)
             if col < Q_SIZE:
@@ -241,10 +248,10 @@ def tile_gemmaattention_pa_kernel(
             nc.vector.memset(plane[:].bitcast(I32), 0)
 
         load_x(0, 1)
-        load_freqs(0, 2)
         load_x(1, 1)
         load_scales(0)
         load_words(0)
+        load_freqs(0, 2)
         load_words(1)
         load_scales(1)
         load_words(2)
@@ -266,9 +273,9 @@ def tile_gemmaattention_pa_kernel(
         )
         for g in range(PASSES):
             quantize([(0, g)], first[g])
-        table_on_vector(0, gains)
         quantize([(1, g) for g in range(PASSES)], second)
-        table_on_vector(1, gains)
+        for i in range(2):
+            table_on_vector(i, gains)
 
         pending = []
         for i, col, heads in [(0, 0, 1), (0, HD, 1), (1, 0, 2)]:
@@ -295,7 +302,7 @@ def tile_gemmaattention_pa_kernel(
                 side += [(values, a + t, c) for t in range(2) for c in range(2)]
                 side += [None] * (2 * STEPS - len(side))
             else:
-                grouped = new_grouped(2 * PASSES)
+                grouped = shared_tile([P, 2 * HIDDEN], BF16)
                 side += [(turn_x, a + 2 + t, 0, PASSES, grouped[:, t * HIDDEN : (t + 1) * HIDDEN]) for t in range(2)]
                 side += [(turn_freqs, a + 2)]
                 side += [(make, a + 2 + t) for t in range(2) for make in (cos_factors, sin_factors)]
@@ -325,9 +332,10 @@ def tile_gemmaattention_pa_kernel(
                     if t >= on_gpsimd:
                         tail.append((a + t, col, terms[:, t : t + 1, :, :, :]))
                     elif t == on_gpsimd - 1:
-                        if b == QUANTISE_STEP and not last:
+                        quantises = b == QUANTISE_STEP and not last
+                        if quantises:
                             quantize([(a + 2 + j, g) for j in range(2) for g in range(PASSES)], grouped)
-                        add(nc.gpsimd, a, col, terms[:, :on_gpsimd, :, :, :])
+                        add(nc.gpsimd, a, col, terms[:, :on_gpsimd, :, :, :], quantises)
 
         i, col, terms = tail[-1]
         tail = tail[:-1] + [(i, col + h * HD, terms[:, :, h : h + 1, :, :]) for h in range(2)]

from contextlib import ExitStack

import concourse.mybir as mybir
from concourse.masks import make_identity

F32 = mybir.dt.float32
BF16 = mybir.dt.bfloat16
I32 = mybir.dt.int32
U32 = mybir.dt.uint32
U8 = mybir.dt.uint8
E5M2X4 = mybir.dt.float8_e5m2_x4
E2M1X4 = mybir.dt.float4_e2m1fn_x4
ALU = mybir.AluOpType
ACT = mybir.ActivationFunctionType

S, HIDDEN, HD = 1024, 1024, 256
Q_SIZE, KV_SIZE = 2048, 1024
O_SIZE = Q_SIZE + 2 * KV_SIZE
EPS = 1e-6
FLOPS = 2 * S * HIDDEN * O_SIZE

P = 128
HALF = HD // 2
TILES = S // P
PASSES = HIDDEN // 512
BANK = 512
STEPS = (Q_SIZE + KV_SIZE) // BANK
QK_BANKS = 5
QUANTISE_STEP = 3
VECTOR_TAIL = 3
WORD_CHUNKS = [(0, 512), (512, 512), (1024, 1024), (2048, 1024), (3072, 1024)]
SCALE_CHUNKS = [(0, 1024), (1024, 2048), (3072, 1024)]


def tile_gemmaattention_pa_kernel(
    tc, x, qkv_w_words, qkv_w_scales, q_norm_w, k_norm_w, freqs_cos, freqs_sin, out_0, out_1, out_2
):
    nc = tc.nc
    x_rows = x[0].rearrange("(p i) k -> p i k", i=TILES)
    cos_rows = freqs_cos.rearrange("(p i) d -> p i d", i=TILES)
    sin_rows = freqs_sin.rearrange("(p i) d -> p i d", i=TILES)
    q_rows = out_0[0].rearrange("(p i) h d -> p i (h d)", i=TILES)
    k_rows = out_1[0].rearrange("(p i) h d -> p i (h d)", i=TILES)
    v_rows = out_2[0].rearrange("(p i) h d -> p i (h d)", i=TILES)

    with ExitStack() as ctx:
        keep = ctx.enter_context(tc.tile_pool(name="keep", bufs=1))
        work = ctx.enter_context(tc.tile_pool(name="work", bufs=3))
        psum = ctx.enter_context(tc.psum_pool(name="psum", bufs=1))
        ctx.enter_context(tc.manual_schedule())

        ident = keep.tile([P, P], F32, name="ident")
        ident4 = keep.tile([P, 4 * P], BF16, name="ident4")
        ones = keep.tile([P, P], BF16, name="ones")
        gain_rows = keep.tile([P, 2 * HD], BF16, name="gain_rows")
        diag_w = keep.tile([P, 4 * P], BF16, name="diag_w")
        planes = [keep.tile([P, PASSES, n], U8, name="plane%d" % c0, align_bytes=64) for c0, n in SCALE_CHUNKS]
        words = [keep.tile([P, PASSES, 2 * n], U8, name="words%d" % c0, align_bytes=64) for c0, n in WORD_CHUNKS]
        tables = [keep.tile([P, 2, 4, HALF], F32, name="table%d" % i) for i in range(TILES)]
        x_sb = {}
        freq_sb = {}
        freq_t = {}
        x_mx = {}
        v_out = {}
        stores = []

        def qk_bank():
            return psum.tile([P, BANK], F32, name="qk", tag="qk", bufs=QK_BANKS)

        def side_bank(shape, dtype):
            return psum.tile(shape, dtype, name="side", tag="side", bufs=8 - QK_BANKS)

        def load_x(i0, n):
            rows = keep.tile([P, n, HIDDEN], BF16, name="x%d" % i0)
            nc.sync.dma_start(out=rows[:], in_=x_rows[:, i0 : i0 + n, :])
            for t in range(n):
                x_sb[i0 + t] = rows[:, t, :]

        def load_freqs(i0, n):
            cos = keep.tile([P, n, HALF], BF16, name="cos%d" % i0)
            sin = keep.tile([P, n, HALF], BF16, name="sin%d" % i0)
            nc.sync.dma_start(out=cos[:], in_=cos_rows[:, i0 : i0 + n, :])
            nc.sync.dma_start(out=sin[:], in_=sin_rows[:, i0 : i0 + n, :])
            for t in range(n):
                freq_sb[i0 + t] = (cos[:, t, :], sin[:, t, :])

        def load_words(c):
            c0, n = WORD_CHUNKS[c]
            src = qkv_w_words.rearrange("g p b -> p g b")[:, :, 2 * c0 : 2 * (c0 + n)]
            nc.sync.dma_start(out=words[c][:].bitcast(I32), in_=src.bitcast(I32))

        def load_scales(c):
            c0, n = SCALE_CHUNKS[c]
            for r in range(4):
                src = qkv_w_scales[:, r:16:4, c0 : c0 + n].rearrange("g q n -> q g n")
                nc.sync.dma_start(out=planes[c][r:P:32, :, :].bitcast(I32), in_=src.bitcast(I32))

        def chunk_of(tiles, chunks, col):
            return [(t, col - c0) for t, (c0, n) in zip(tiles, chunks) if c0 <= col < c0 + n][0]

        def project(i, col, width, bank):
            word_tile, w0 = chunk_of(words, WORD_CHUNKS, col)
            plane, s0 = chunk_of(planes, SCALE_CHUNKS, col)
            for g in range(PASSES):
                codes, scales = x_mx[i, g]
                nc.tensor.matmul_mx(
                    out=bank[:, :width],
                    lhsT=codes.bitcast(E5M2X4),
                    lhsT_scale=scales,
                    rhs=word_tile[:, g, 2 * w0 : 2 * (w0 + width)].bitcast(E2M1X4),
                    rhs_scale=plane[:, g, s0 : s0 + width],
                    start=(g == 0),
                    stop=(g == PASSES - 1),
                )

        def turn_x(i, g0, n, grouped):
            pairs = x_sb[i].bitcast(F32)
            bank = side_bank([P, n, 2, P], F32)
            for g in range(n):
                for u in range(2):
                    w0 = 256 * (g0 + g)
                    nc.tensor.transpose(bank[:, g, u, :], pairs[:, w0 + u : w0 + 256 : 2], ident[:])
            nc.scalar.copy(
                out=grouped.bitcast(F32).rearrange("p (g r u) -> p g r u", g=n, u=2),
                in_=bank[:].rearrange("p g u r -> p g r u"),
            )

        def new_grouped(n):
            return work.tile([P, n * 4 * P], BF16, name="grouped", tag="grouped", align_bytes=64)

        def shared_tile(shape, dtype):
            return work.tile(shape, dtype, name="shared", tag="shared", align_bytes=64, bufs=1)

        def quantize(keys, grouped):
            n = len(keys)
            codes = work.tile([P, n * P], U32, name="codes", tag="codes", align_bytes=64, bufs=5)
            scales = work.tile([P, n * P], U8, name="scales", tag="scales", align_bytes=64, bufs=5)
            nc.vector.quantize_mx(out=codes[:].bitcast(E5M2X4), scales=scales[:], in_=grouped[:])
            for j, key in enumerate(keys):
                x_mx[key] = (codes[:, j * P : (j + 1) * P], scales[:, j * P : (j + 1) * P])

        def turn_freqs(a):
            sources = freq_sb[a] + freq_sb[a + 1]
            bank = side_bank([P, 4, P], BF16)
            for j, src in enumerate(sources):
                nc.tensor.transpose(bank[:, j, :], src, ident4[:, :P])
            turned = keep.tile([P, 4, P], BF16, name="freq_t%d" % a)
            nc.scalar.copy(out=turned[:], in_=bank[:])
            for t in range(2):
                freq_t[a + t] = (turned[:, 2 * t, :], turned[:, 2 * t + 1, :])

        def times_gains(turned):
            bank = side_bank([P, 2, 2, HALF], F32)
            flat = bank[:].rearrange("p t h d -> p (t h d)")
            nc.tensor.matmul(flat, lhsT=turned, rhs=ident4[:], start=True, stop=False)
            nc.tensor.matmul(flat, lhsT=turned, rhs=diag_w[:], start=False, stop=True)
            return bank

        def cos_factors(i):
            bank = times_gains(freq_t[i][0])
            nc.scalar.copy(out=tables[i][:, :, 0:4:3, :], in_=bank[:])

        def sin_factors(i):
            bank = times_gains(freq_t[i][1])
            nc.scalar.copy(out=tables[i][:, :, 2, :], in_=bank[:, :, 0, :])
            nc.scalar.activation(out=tables[i][:, :, 1, :], in_=bank[:, :, 1, :], func=ACT.Copy, scale=-1.0)

        def table_on_vector(i, gains):
            gains4 = gains[:].rearrange("p (t h d) -> p t h d", t=2, h=2)
            c = freq_sb[i][0].unsqueeze(1).unsqueeze(1).to_broadcast([P, 2, 2, HALF])
            s = freq_sb[i][1].unsqueeze(1).to_broadcast([P, 2, HALF])
            nc.vector.tensor_tensor(out=tables[i][:, :, 0:4:3, :], in0=gains4, in1=c, op=ALU.mult)
            nc.vector.tensor_tensor(out=tables[i][:, :, 2, :], in0=gains4[:, :, 0, :], in1=s, op=ALU.mult)
            nc.vector.scalar_tensor_tensor(
                out=tables[i][:, :, 1, :], in0=gains4[:, :, 1, :], scalar=-1.0, in1=s, op0=ALU.mult, op1=ALU.mult
            )

        def values(i, c):
            if c == 0:
                v_out[i] = work.tile([P, KV_SIZE], F32, name="v_out", tag="v_out", bufs=4)
            bank = side_bank([P, BANK], F32)
            project(i, Q_SIZE + KV_SIZE + c * BANK, BANK, bank)
            nc.scalar.copy(out=v_out[i][:, c * BANK : (c + 1) * BANK], in_=bank[:])
            if c == 1:
                nc.sync.dma_start(out=v_rows[:, i, :], in_=v_out[i][:])

        def new_sums(heads):
            return work.tile([P, heads], F32, name="sums", tag="sums", bufs=4)

        def square(bank, h, sums):
            squares = work.tile([P, HD], BF16, name="squares", tag="squares")
            nc.scalar.activation(
                out=squares[:], in_=bank[:, h * HD : (h + 1) * HD], func=ACT.Square, accum_out=sums[:, h : h + 1]
            )

        def inverse_rms(sums):
            rstd = work.tile([P, sums.shape[1]], F32, name="rstd", tag="rstd", bufs=4)
            nc.scalar.activation(out=rstd[:], in_=sums[:], func=ACT.Abs_reciprocal_sqrt, scale=1.0 / HD, bias=EPS)
            return rstd

        def new_terms(tiles, heads):
            return work.tile([P, tiles, heads, 2, HD], F32, name="terms", tag="terms", bufs=5)

        def multiply(i, col, bank, h, rstd, terms):
            table = tables[i][:, 0 if col < Q_SIZE else 1, :, :].rearrange("p (j h) d -> p j (h d)", j=2)
            u = bank[:, h * HD : (h + 1) * HD].unsqueeze(1).to_broadcast([P, 2, HD])
            nc.vector.scalar_tensor_tensor(out=terms, in0=u, scalar=rstd, in1=table, op0=ALU.mult, op1=ALU.mult)

        def add(engine, i, col, terms, after_quantise=False):
            tiles, heads = terms.shape[1], terms.shape[2]
            shape = [P, tiles * heads * 2, HALF]
            if after_quantise:
                result = shared_tile(shape, F32)
            else:
                result = work.tile(shape, F32, name="result", tag="result", bufs=8)
            halves = terms.rearrange("p t n j (h d) -> p (t n j) h d", h=2)
            engine.tensor_tensor(out=result[:], in0=halves[:, :, 0, :], in1=halves[:, :, 1, :], op=ALU.add)
            if col < Q_SIZE:
                dst = q_rows[:, i : i + tiles, col : col + heads * HD]
            else:
                dst = k_rows[:, i : i + tiles, col - Q_SIZE : col - Q_SIZE + heads * HD]
            stores.append((dst, result[:].rearrange("p (t n) d -> p t (n d)", t=tiles)))

        def flush(keep_last):
            while len(stores) > keep_last:
                dst, src = stores[0]
                nc.sync.dma_start(out=dst, in_=src)
                stores.remove(stores[0])

        def finish_unit(i, col, heads, sums, bank):
            rstd = inverse_rms(sums)
            terms = new_terms(1, heads)
            for h in range(heads):
                multiply(i, col, bank, h, rstd[:, h : h + 1], terms[:, 0, h, :, :])
            add(nc.gpsimd, i, col, terms[:])

        nc.scalar.dma_start(out=gain_rows[P - 1 : P, 0:HD], in_=q_norm_w.rearrange("(o d) -> o d", o=1))
        nc.scalar.dma_start(out=gain_rows[P - 1 : P, HD : 2 * HD], in_=k_norm_w.rearrange("(o d) -> o d", o=1))
        nc.vector.memset(planes[0][:].bitcast(I32), 0)
        nc.vector.memset(gain_rows[: P - 1, :], 0.0)
        nc.vector.memset(ones[:], 1.0)
        nc.vector.memset(gain_rows[0:1, :], 1.0)
        make_identity(nc, ident[:])
        nc.vector.tensor_copy(
            out=ident4[:].rearrange("p (c d) -> p c d", c=4), in_=ident[:].unsqueeze(1).to_broadcast([P, 4, P])
        )
        for plane in planes[1:]:
            nc.vector.memset(plane[:].bitcast(I32), 0)

        load_x(0, 1)
        load_x(1, 1)
        load_scales(0)
        load_words(0)
        load_freqs(0, 2)
        load_words(1)
        load_scales(1)
        load_words(2)
        load_x(2, 2)
        load_freqs(2, TILES - 2)
        load_words(3)
        load_scales(2)
        load_words(4)

        gains = qk_bank()
        nc.tensor.matmul(gains[:], lhsT=ones[:], rhs=gain_rows[:], start=True, stop=True)
        first = [new_grouped(1) for g in range(PASSES)]
        second = new_grouped(PASSES)
        for g in range(PASSES):
            turn_x(0, g, 1, first[g][:])
        turn_x(1, 0, PASSES, second[:])
        nc.vector.scalar_tensor_tensor(
            out=diag_w[:], in0=gains[:], scalar=-1.0, in1=ident4[:], op0=ALU.add, op1=ALU.mult
        )
        for g in range(PASSES):
            quantize([(0, g)], first[g])
        quantize([(1, g) for g in range(PASSES)], second)
        for i in range(2):
            table_on_vector(i, gains)

        pending = []
        for i, col, heads in [(0, 0, 1), (0, HD, 1), (1, 0, 2)]:
            sums = new_sums(heads)
            bank = qk_bank()
            project(i, col, heads * HD, bank)
            for h in range(heads):
                square(bank, h, sums)
                for unit in pending:
                    finish_unit(*unit)
                pending = []
            pending = [(i, col, heads, sums, bank)]
            if col == 0 and i == 0:
                finish_unit(*pending[0])
                pending = []

        for a in range(0, TILES, 2):
            last = a == TILES - 2
            if a + 4 < TILES:
                load_x(a + 4, 2)
            side = [None]
            side += [(values, a - 2 + t, c) if a > 0 else None for t in range(2) for c in range(2)]
            if last:
                side += [(values, a + t, c) for t in range(2) for c in range(2)]
                side += [None] * (2 * STEPS - len(side))
            else:
                grouped = shared_tile([P, 2 * HIDDEN], BF16)
                side += [(turn_x, a + 2 + t, 0, PASSES, grouped[:, t * HIDDEN : (t + 1) * HIDDEN]) for t in range(2)]
                side += [(turn_freqs, a + 2)]
                side += [(make, a + 2 + t) for t in range(2) for make in (cos_factors, sin_factors)]
            tail = []
            for b in range(1 if a == 0 else 0, STEPS):
                col = b * BANK
                sums = new_sums(4)
                banks = []
                for t in range(2):
                    banks.append(qk_bank())
                    project(a + t, col, BANK, banks[t])
                    for h in range(2):
                        square(banks[t], h, sums[:, 2 * t : 2 * t + 2])
                        for unit in pending:
                            finish_unit(*unit)
                        pending = []
                    job = side[2 * b + t]
                    if job is not None:
                        job[0](*job[1:])
                rstd = inverse_rms(sums)
                flush(1)
                terms = new_terms(2, 2)
                on_gpsimd = min(2, max(0, 2 * STEPS - VECTOR_TAIL - 2 * b)) if last else 2
                for t in range(2):
                    for h in range(2):
                        multiply(a + t, col, banks[t], h, rstd[:, 2 * t + h : 2 * t + h + 1], terms[:, t, h, :, :])
                    if t >= on_gpsimd:
                        tail.append((a + t, col, terms[:, t : t + 1, :, :, :]))
                    elif t == on_gpsimd - 1:
                        quantises = b == QUANTISE_STEP and not last
                        if quantises:
                            quantize([(a + 2 + j, g) for j in range(2) for g in range(PASSES)], grouped)
                        add(nc.gpsimd, a, col, terms[:, :on_gpsimd, :, :, :], quantises)

        i, col, terms = tail[-1]
        tail = tail[:-1] + [(i, col + h * HD, terms[:, :, h : h + 1, :, :]) for h in range(2)]
        for part in tail:
            add(nc.vector, *part)
            flush(0)
